import numpy as np
import ml_dtypes

BF16 = ml_dtypes.bfloat16


def bf(x):
    return np.asarray(x, np.float32).astype(BF16)


def f32(x):
    return np.asarray(x, np.float32)


def f64(x):
    return np.asarray(x).astype(np.float64)


def striped(idx):
    return np.tile(idx.reshape(-1, 16).T, (8, 1))


S, D, CH, M, N = 512, 128, 4, 512, 256
EPS = 1e-5
BN1_G, BN1_B, BN1_M, BN1_V = 1.2, -0.15, 0.2, 0.8


def taps():
    return np.random.uniform(0.4, 1.0, CH) * np.random.choice([-1.0, 1.0], CH)


def setup_inputs():
    table = bf(np.random.standard_normal((S, D)))
    w0 = bf(np.kron(taps()[None, :], np.eye(D)))
    rel = bf(np.random.standard_normal((D, N)))
    w1 = bf(np.kron(taps()[None, :], np.eye(D)))
    cb = f32(np.repeat(0.3 * np.random.standard_normal(CH), D)[:, None])
    fc_w = bf(np.random.standard_normal((M, D)) / np.sqrt(M))
    fc_b = f32(0.1 * np.random.standard_normal((D, 1)))
    bn3_gain = f32(np.random.uniform(0.5, 1.5, (D, 1)))
    bn3_bias = f32(0.1 * np.random.standard_normal((D, 1)))
    bn3_mean = f32(0.1 * np.random.standard_normal((D, 1)))
    bn3_var = f32(np.random.uniform(0.5, 1.5, (D, 1)))
    idx = np.random.permutation(np.tile(np.arange(S), 2))[:N]
    return {"table": table, "w0": w0, "rel": rel, "w1": w1, "cb": cb, "fc_w": fc_w, "fc_b": fc_b, "bn3_gain": bn3_gain, "bn3_bias": bn3_bias, "bn3_mean": bn3_mean, "bn3_var": bn3_var, "offs": striped(idx)}


def reference(table, w0, rel, w1, cb, fc_w, fc_b, bn3_gain, bn3_bias, bn3_mean, bn3_var, offs):
    idx = offs[:16].T.reshape(-1)
    s1 = BN1_G / np.sqrt(BN1_V + EPS)
    tn = (f64(table) - BN1_M) * s1 + BN1_B
    rn = (f64(rel) - BN1_M) * s1 + BN1_B
    feat = np.maximum(f64(w0).T @ tn[idx].T + f64(w1).T @ rn + f64(cb), 0.0)
    z = f64(fc_w).T @ feat + f64(fc_b)
    z = (z - f64(bn3_mean)) * (f64(bn3_gain) / np.sqrt(f64(bn3_var) + EPS)) + f64(bn3_bias)
    return np.maximum(z, 0.0)

@@ -1,0 +1,102 @@
+import math
+
+import concourse.mybir as mybir
+from concourse.masks import make_identity
+
+P = 128
+S = 512
+CH = 4
+N = 256
+EPS = 1e-5
+
+S1 = 1.2 / math.sqrt(0.8 + EPS)
+SHIFT1 = -0.2 * S1 - 0.15
+
+FLOPS = 2 * N * P * (CH * P) * 3
+
+BF16 = mybir.dt.bfloat16
+F32 = mybir.dt.float32
+U16 = mybir.dt.uint16
+ALU = mybir.AluOpType
+ACT = mybir.ActivationFunctionType
+
+
+def tile_conve_kernel(
+    tc, table, w0, rel, w1, cb, fc_w, fc_b, bn3_gain, bn3_bias, bn3_mean, bn3_var, offs, out
+):
+    nc = tc.nc
+    with tc.tile_pool(name="held", bufs=1) as held, tc.psum_pool(name="psum", bufs=1) as psum:
+        table_sb = held.tile([P, S // P, P], BF16)
+        nc.sync.dma_start(table_sb[:], table.rearrange("(a p) k -> p a k", p=P))
+        rel_sb = held.tile([P, N], BF16)
+        nc.scalar.dma_start(rel_sb[:], rel)
+        offsets = held.tile([P, N // 16], U16)
+        nc.sync.dma_start(offsets[:], offs)
+        w1_sb = held.tile([P, CH * P], BF16)
+        nc.scalar.dma_start(w1_sb[:], w1)
+        w0_sb = held.tile([P, CH * P], BF16)
+        nc.sync.dma_start(w0_sb[:], w0)
+        cb_sb = held.tile([P, CH], F32)
+        with nc.allow_non_contiguous_dma(reason="512 biases, one to a partition and block"):
+            nc.scalar.dma_start(cb_sb[:], cb.rearrange("(c d) o -> d (c o)", d=P))
+        fc_w_sb = held.tile([P, CH, P], BF16)
+        nc.sync.dma_start(fc_w_sb[:], fc_w.rearrange("(c p) d -> p c d", p=P))
+        var_sb = held.tile([P, 1], F32)
+        nc.scalar.dma_start(var_sb[:], bn3_var)
+        gain_sb = held.tile([P, 1], F32)
+        nc.sync.dma_start(gain_sb[:], bn3_gain)
+        fc_b_sb = held.tile([P, 1], F32)
+        nc.scalar.dma_start(fc_b_sb[:], fc_b)
+        mean_sb = held.tile([P, 1], F32)
+        nc.sync.dma_start(mean_sb[:], bn3_mean)
+        bias_sb = held.tile([P, 1], F32)
+        nc.scalar.dma_start(bias_sb[:], bn3_bias)
+
+        identity = held.tile([P, P], BF16)
+        make_identity(nc, identity[:])
+
+        minus_half = held.tile([P, 1], F32)
+        nc.gpsimd.memset(minus_half[:], -0.5)
+        var_eps = held.tile([P, 1], F32)
+        nc.gpsimd.tensor_scalar(var_eps[:], var_sb[:], EPS, None, ALU.add)
+        rstd = held.tile([P, 1], F32)
+        nc.gpsimd.tensor_tensor(rstd[:], var_eps[:], minus_half[:], ALU.pow)
+        scale3 = held.tile([P, 1], F32)
+        nc.gpsimd.tensor_tensor(scale3[:], gain_sb[:], rstd[:], ALU.mult)
+        centred = held.tile([P, 1], F32)
+        nc.gpsimd.tensor_tensor(centred[:], fc_b_sb[:], mean_sb[:], ALU.subtract)
+        scaled = held.tile([P, 1], F32)
+        nc.gpsimd.tensor_tensor(scaled[:], centred[:], scale3[:], ALU.mult)
+        shift3 = held.tile([P, 1], F32)
+        nc.gpsimd.tensor_tensor(shift3[:], scaled[:], bias_sb[:], ALU.add)
+
+        flipped = psum.tile([P, S], BF16)
+        for a in range(S // P):
+            nc.tensor.transpose(flipped[:, a * P : (a + 1) * P], table_sb[:, a, :], identity[:])
+        tn = held.tile([P, S], BF16)
+        nc.vector.tensor_scalar(tn[:], flipped[:], S1, SHIFT1, ALU.mult, ALU.add)
+
+        rn = held.tile([P, N], BF16)
+        nc.vector.tensor_scalar(rn[:], rel_sb[:], S1, SHIFT1, ALU.mult, ALU.add)
+
+        feat_ps = [psum.tile([P, N], F32, name=f"feat_ps{c}") for c in range(CH)]
+        for c in range(CH):
+            nc.tensor.matmul(feat_ps[c][:], w1_sb[:, c * P : (c + 1) * P], rn[:], start=True, stop=False)
+        for c in range(CH):
+            nc.tensor.matmul(
+                feat_ps[c][:], w0_sb[:, c * P : (c + 1) * P], tn[:].indirect(offsets[:]), start=False, stop=True
+            )
+
+        feat = [held.tile([P, N], BF16, name=f"feat{c}") for c in range(CH)]
+        for c in range(CH):
+            if c % 2 == 0:
+                nc.scalar.activation(feat[c][:], feat_ps[c][:], ACT.Relu, bias=cb_sb[:, c : c + 1], scale=1.0)
+            else:
+                nc.vector.tensor_scalar(feat[c][:], feat_ps[c][:], cb_sb[:, c : c + 1], 0.0, ALU.add, ALU.max)
+
+        z_ps = psum.tile([P, N], F32)
+        for c in range(CH):
+            nc.tensor.matmul(z_ps[:], fc_w_sb[:, c, :], feat[c][:], start=(c == 0), stop=(c == CH - 1))
+        out_sb = held.tile([P, N], F32)
+        nc.scalar.activation(out_sb[:], z_ps[:], ACT.Relu, bias=shift3[:], scale=scale3[:])
+        nc.sync.dma_start(out, out_sb[:])

@@ -12,6 +12,9 @@ EPS = 1e-5
 S1 = 1.2 / math.sqrt(0.8 + EPS)
 SHIFT1 = -0.2 * S1 - 0.15
 
+WARM_COLUMNS = 512
+WARM_MATMULS = 5
+
 FLOPS = 2 * N * P * (CH * P) * 3
 
 BF16 = mybir.dt.bfloat16
@@ -54,6 +57,12 @@ def tile_conve_kernel(
 
         identity = held.tile([P, P], BF16)
         make_identity(nc, identity[:])
+
+        zeros = held.tile([P, WARM_COLUMNS], BF16)
+        nc.vector.memset(zeros[:], 0.0)
+        warm_ps = psum.tile([P, WARM_COLUMNS], F32)
+        for w in range(WARM_MATMULS):
+            nc.tensor.matmul(warm_ps[:], zeros[:, 0:P], zeros[:], start=True, stop=True)
 
         minus_half = held.tile([P, 1], F32)
         nc.gpsimd.memset(minus_half[:], -0.5)

@@ -11,9 +11,8 @@ EPS = 1e-5
 
 S1 = 1.2 / math.sqrt(0.8 + EPS)
 SHIFT1 = -0.2 * S1 - 0.15
-
-WARM_COLUMNS = 512
-WARM_MATMULS = 5
+BLOCKS = S // P
+assert BLOCKS == CH
 
 FLOPS = 2 * N * P * (CH * P) * 3
 
@@ -29,7 +28,7 @@ def tile_conve_kernel(
 ):
     nc = tc.nc
     with tc.tile_pool(name="held", bufs=1) as held, tc.psum_pool(name="psum", bufs=1) as psum:
-        table_sb = held.tile([P, S // P, P], BF16)
+        table_sb = held.tile([P, BLOCKS, P], BF16)
         nc.sync.dma_start(table_sb[:], table.rearrange("(a p) k -> p a k", p=P))
         rel_sb = held.tile([P, N], BF16)
         nc.scalar.dma_start(rel_sb[:], rel)
@@ -55,17 +54,31 @@ def tile_conve_kernel(
         bias_sb = held.tile([P, 1], F32)
         nc.scalar.dma_start(bias_sb[:], bn3_bias)
 
+        minus_half = held.tile([P, 1], F32)
+        nc.gpsimd.memset(minus_half[:], -0.5)
         identity = held.tile([P, P], BF16)
         make_identity(nc, identity[:])
 
-        zeros = held.tile([P, WARM_COLUMNS], BF16)
-        nc.vector.memset(zeros[:], 0.0)
-        warm_ps = psum.tile([P, WARM_COLUMNS], F32)
-        for w in range(WARM_MATMULS):
-            nc.tensor.matmul(warm_ps[:], zeros[:, 0:P], zeros[:], start=True, stop=True)
+        scratch = held.tile([P, 1], F32)
+        nc.scalar.activation(scratch[:], minus_half[:], ACT.Relu)
 
-        minus_half = held.tile([P, 1], F32)
-        nc.gpsimd.memset(minus_half[:], -0.5)
+        rn = held.tile([P, N], BF16)
+        nc.vector.tensor_scalar(rn[:], rel_sb[:], S1, SHIFT1, ALU.mult, ALU.add)
+
+        tn = held.tile([P, S], BF16)
+        for a in range(BLOCKS):
+            flipped = psum.tile([P, P], BF16, name=f"flipped{a}", tag=f"bank{a}")
+            nc.tensor.transpose(flipped[:], table_sb[:, a, :], identity[:])
+            nc.vector.tensor_scalar(tn[:, a * P : (a + 1) * P], flipped[:], S1, SHIFT1, ALU.mult, ALU.add)
+
+        feat_ps = [psum.tile([P, N], F32, name=f"feat_ps{c}", tag=f"bank{c}") for c in range(CH)]
+        for c in range(CH):
+            nc.tensor.matmul(feat_ps[c][:], w1_sb[:, c * P : (c + 1) * P], rn[:], start=True, stop=False)
+        for c in range(CH):
+            nc.tensor.matmul(
+                feat_ps[c][:], w0_sb[:, c * P : (c + 1) * P], tn[:].indirect(offsets[:]), start=False, stop=True
+            )
+
         var_eps = held.tile([P, 1], F32)
         nc.gpsimd.tensor_scalar(var_eps[:], var_sb[:], EPS, None, ALU.add)
         rstd = held.tile([P, 1], F32)
@@ -78,23 +91,6 @@ def tile_conve_kernel(
         nc.gpsimd.tensor_tensor(scaled[:], centred[:], scale3[:], ALU.mult)
         shift3 = held.tile([P, 1], F32)
         nc.gpsimd.tensor_tensor(shift3[:], scaled[:], bias_sb[:], ALU.add)
-
-        flipped = psum.tile([P, S], BF16)
-        for a in range(S // P):
-            nc.tensor.transpose(flipped[:, a * P : (a + 1) * P], table_sb[:, a, :], identity[:])
-        tn = held.tile([P, S], BF16)
-        nc.vector.tensor_scalar(tn[:], flipped[:], S1, SHIFT1, ALU.mult, ALU.add)
-
-        rn = held.tile([P, N], BF16)
-        nc.vector.tensor_scalar(rn[:], rel_sb[:], S1, SHIFT1, ALU.mult, ALU.add)
-
-        feat_ps = [psum.tile([P, N], F32, name=f"feat_ps{c}") for c in range(CH)]
-        for c in range(CH):
-            nc.tensor.matmul(feat_ps[c][:], w1_sb[:, c * P : (c + 1) * P], rn[:], start=True, stop=False)
-        for c in range(CH):
-            nc.tensor.matmul(
-                feat_ps[c][:], w0_sb[:, c * P : (c + 1) * P], tn[:].indirect(offsets[:]), start=False, stop=True
-            )
 
         feat = [held.tile([P, N], BF16, name=f"feat{c}") for c in range(CH)]
         for c in range(CH):

@@ -13,6 +13,8 @@ S1 = 1.2 / math.sqrt(0.8 + EPS)
 SHIFT1 = -0.2 * S1 - 0.15
 BLOCKS = S // P
 assert BLOCKS == CH
+WARM_COLUMNS = 512
+WARM_MATMULS = 3
 
 FLOPS = 2 * N * P * (CH * P) * 3
 
@@ -34,23 +36,23 @@ def tile_conve_kernel(
         nc.scalar.dma_start(rel_sb[:], rel)
         offsets = held.tile([P, N // 16], U16)
         nc.sync.dma_start(offsets[:], offs)
-        w1_sb = held.tile([P, CH * P], BF16)
-        nc.scalar.dma_start(w1_sb[:], w1)
+        var_sb = held.tile([P, 1], F32)
+        nc.scalar.dma_start(var_sb[:], bn3_var)
         w0_sb = held.tile([P, CH * P], BF16)
         nc.sync.dma_start(w0_sb[:], w0)
+        w1_sb = held.tile([P, CH * P], BF16)
+        nc.scalar.dma_start(w1_sb[:], w1)
+        gain_sb = held.tile([P, 1], F32)
+        nc.sync.dma_start(gain_sb[:], bn3_gain)
         cb_sb = held.tile([P, CH], F32)
         with nc.allow_non_contiguous_dma(reason="512 biases, one to a partition and block"):
             nc.scalar.dma_start(cb_sb[:], cb.rearrange("(c d) o -> d (c o)", d=P))
-        fc_w_sb = held.tile([P, CH, P], BF16)
-        nc.sync.dma_start(fc_w_sb[:], fc_w.rearrange("(c p) d -> p c d", p=P))
-        var_sb = held.tile([P, 1], F32)
-        nc.scalar.dma_start(var_sb[:], bn3_var)
-        gain_sb = held.tile([P, 1], F32)
-        nc.sync.dma_start(gain_sb[:], bn3_gain)
-        fc_b_sb = held.tile([P, 1], F32)
-        nc.scalar.dma_start(fc_b_sb[:], fc_b)
         mean_sb = held.tile([P, 1], F32)
         nc.sync.dma_start(mean_sb[:], bn3_mean)
+        fc_b_sb = held.tile([P, 1], F32)
+        nc.scalar.dma_start(fc_b_sb[:], fc_b)
+        fc_w_sb = held.tile([P, CH, P], BF16)
+        nc.sync.dma_start(fc_w_sb[:], fc_w.rearrange("(c p) d -> p c d", p=P))
         bias_sb = held.tile([P, 1], F32)
         nc.scalar.dma_start(bias_sb[:], bn3_bias)
 
@@ -61,6 +63,12 @@ def tile_conve_kernel(
 
         scratch = held.tile([P, 1], F32)
         nc.scalar.activation(scratch[:], minus_half[:], ACT.Relu)
+
+        zeros = held.tile([P, WARM_COLUMNS], BF16)
+        nc.vector.memset(zeros[:], 0.0)
+        warm_ps = psum.tile([P, WARM_COLUMNS], F32)
+        for w in range(WARM_MATMULS):
+            nc.tensor.matmul(warm_ps[:], zeros[:, 0:P], zeros[:], start=True, stop=True)
 
         rn = held.tile([P, N], BF16)
         nc.vector.tensor_scalar(rn[:], rel_sb[:], S1, SHIFT1, ALU.mult, ALU.add)
@@ -87,10 +95,8 @@ def tile_conve_kernel(
         nc.gpsimd.tensor_tensor(scale3[:], gain_sb[:], rstd[:], ALU.mult)
         centred = held.tile([P, 1], F32)
         nc.gpsimd.tensor_tensor(centred[:], fc_b_sb[:], mean_sb[:], ALU.subtract)
-        scaled = held.tile([P, 1], F32)
-        nc.gpsimd.tensor_tensor(scaled[:], centred[:], scale3[:], ALU.mult)
         shift3 = held.tile([P, 1], F32)
-        nc.gpsimd.tensor_tensor(shift3[:], scaled[:], bias_sb[:], ALU.add)
+        nc.gpsimd.tensor_scalar(shift3[:], centred[:], scale3[:], bias_sb[:], ALU.mult, ALU.add)
 
         feat = [held.tile([P, N], BF16, name=f"feat{c}") for c in range(CH)]
         for c in range(CH):

@@ -33,28 +33,28 @@ def tile_conve_kernel(
         table_sb = held.tile([P, BLOCKS, P], BF16)
         nc.sync.dma_start(table_sb[:], table.rearrange("(a p) k -> p a k", p=P))
         rel_sb = held.tile([P, N], BF16)
-        nc.scalar.dma_start(rel_sb[:], rel)
+        nc.sync.dma_start(rel_sb[:], rel)
+        w1_sb = held.tile([P, CH * P], BF16)
+        nc.sync.dma_start(w1_sb[:], w1)
         offsets = held.tile([P, N // 16], U16)
         nc.sync.dma_start(offsets[:], offs)
-        var_sb = held.tile([P, 1], F32)
-        nc.scalar.dma_start(var_sb[:], bn3_var)
         w0_sb = held.tile([P, CH * P], BF16)
         nc.sync.dma_start(w0_sb[:], w0)
-        w1_sb = held.tile([P, CH * P], BF16)
-        nc.scalar.dma_start(w1_sb[:], w1)
-        gain_sb = held.tile([P, 1], F32)
-        nc.sync.dma_start(gain_sb[:], bn3_gain)
         cb_sb = held.tile([P, CH], F32)
         with nc.allow_non_contiguous_dma(reason="512 biases, one to a partition and block"):
-            nc.scalar.dma_start(cb_sb[:], cb.rearrange("(c d) o -> d (c o)", d=P))
+            nc.sync.dma_start(cb_sb[:], cb.rearrange("(c d) o -> d (c o)", d=P))
+        fc_w_sb = held.tile([P, CH, P], BF16)
+        nc.sync.dma_start(fc_w_sb[:], fc_w.rearrange("(c p) d -> p c d", p=P))
+        var_sb = held.tile([P, 1], F32)
+        nc.sync.dma_start(var_sb[:], bn3_var)
+        gain_sb = held.tile([P, 1], F32)
+        nc.sync.dma_start(gain_sb[:], bn3_gain)
         mean_sb = held.tile([P, 1], F32)
         nc.sync.dma_start(mean_sb[:], bn3_mean)
         fc_b_sb = held.tile([P, 1], F32)
-        nc.scalar.dma_start(fc_b_sb[:], fc_b)
-        fc_w_sb = held.tile([P, CH, P], BF16)
-        nc.sync.dma_start(fc_w_sb[:], fc_w.rearrange("(c p) d -> p c d", p=P))
+        nc.sync.dma_start(fc_b_sb[:], fc_b)
         bias_sb = held.tile([P, 1], F32)
-        nc.scalar.dma_start(bias_sb[:], bn3_bias)
+        nc.sync.dma_start(bias_sb[:], bn3_bias)
 
         minus_half = held.tile([P, 1], F32)
         nc.gpsimd.memset(minus_half[:], -0.5)
@@ -71,13 +71,16 @@ def tile_conve_kernel(
             nc.tensor.matmul(warm_ps[:], zeros[:, 0:P], zeros[:], start=True, stop=True)
 
         rn = held.tile([P, N], BF16)
-        nc.vector.tensor_scalar(rn[:], rel_sb[:], S1, SHIFT1, ALU.mult, ALU.add)
+        nc.gpsimd.tensor_scalar(rn[:], rel_sb[:], S1, SHIFT1, ALU.mult, ALU.add)
 
         tn = held.tile([P, S], BF16)
         for a in range(BLOCKS):
             flipped = psum.tile([P, P], BF16, name=f"flipped{a}", tag=f"bank{a}")
             nc.tensor.transpose(flipped[:], table_sb[:, a, :], identity[:])
-            nc.vector.tensor_scalar(tn[:, a * P : (a + 1) * P], flipped[:], S1, SHIFT1, ALU.mult, ALU.add)
+            if a % 2 == 0:
+                nc.vector.tensor_scalar(tn[:, a * P : (a + 1) * P], flipped[:], S1, SHIFT1, ALU.mult, ALU.add)
+            else:
+                nc.scalar.activation(tn[:, a * P : (a + 1) * P], flipped[:], ACT.Copy, bias=SHIFT1, scale=S1)
 
         feat_ps = [psum.tile([P, N], F32, name=f"feat_ps{c}", tag=f"bank{c}") for c in range(CH)]
         for c in range(CH):

@@ -7,6 +7,8 @@ P = 128
 S = 512
 CH = 4
 N = 256
+HALVES = 2
+H = N // HALVES
 EPS = 1e-5
 
 S1 = 1.2 / math.sqrt(0.8 + EPS)
@@ -66,7 +68,7 @@ def tile_conve_kernel(
 
         zeros = held.tile([P, WARM_COLUMNS], BF16)
         nc.vector.memset(zeros[:], 0.0)
-        warm_ps = psum.tile([P, WARM_COLUMNS], F32)
+        warm_ps = psum.tile([P, WARM_COLUMNS], F32, tag="bank4")
         for w in range(WARM_MATMULS):
             nc.tensor.matmul(warm_ps[:], zeros[:, 0:P], zeros[:], start=True, stop=True)
 
@@ -82,13 +84,21 @@ def tile_conve_kernel(
             else:
                 nc.scalar.activation(tn[:, a * P : (a + 1) * P], flipped[:], ACT.Copy, bias=SHIFT1, scale=S1)
 
-        feat_ps = [psum.tile([P, N], F32, name=f"feat_ps{c}", tag=f"bank{c}") for c in range(CH)]
-        for c in range(CH):
-            nc.tensor.matmul(feat_ps[c][:], w1_sb[:, c * P : (c + 1) * P], rn[:], start=True, stop=False)
-        for c in range(CH):
-            nc.tensor.matmul(
-                feat_ps[c][:], w0_sb[:, c * P : (c + 1) * P], tn[:].indirect(offsets[:]), start=False, stop=True
-            )
+        feat_ps = [
+            [psum.tile([P, H], F32, name=f"feat_ps{h}_{c}", tag=f"bank{h * CH + c}") for c in range(CH)]
+            for h in range(HALVES)
+        ]
+        for h in range(HALVES):
+            for c in range(CH):
+                nc.tensor.matmul(
+                    feat_ps[h][c][:], w1_sb[:, c * P : (c + 1) * P], rn[:, h * H : (h + 1) * H], start=True, stop=False
+                )
+        for h in range(HALVES):
+            half_offsets = offsets[:, h * (H // 16) : (h + 1) * (H // 16)]
+            for c in range(CH):
+                nc.tensor.matmul(
+                    feat_ps[h][c][:], w0_sb[:, c * P : (c + 1) * P], tn[:].indirect(half_offsets), start=False, stop=True
+                )
 
         var_eps = held.tile([P, 1], F32)
         nc.gpsimd.tensor_scalar(var_eps[:], var_sb[:], EPS, None, ALU.add)
@@ -101,16 +111,21 @@ def tile_conve_kernel(
         shift3 = held.tile([P, 1], F32)
         nc.gpsimd.tensor_scalar(shift3[:], centred[:], scale3[:], bias_sb[:], ALU.mult, ALU.add)
 
-        feat = [held.tile([P, N], BF16, name=f"feat{c}") for c in range(CH)]
-        for c in range(CH):
-            if c % 2 == 0:
-                nc.scalar.activation(feat[c][:], feat_ps[c][:], ACT.Relu, bias=cb_sb[:, c : c + 1], scale=1.0)
-            else:
-                nc.vector.tensor_scalar(feat[c][:], feat_ps[c][:], cb_sb[:, c : c + 1], 0.0, ALU.add, ALU.max)
+        feat = [[held.tile([P, H], BF16, name=f"feat{h}_{c}") for c in range(CH)] for h in range(HALVES)]
+        for h in range(HALVES):
+            for c in range(CH):
+                if c % 2 == 0:
+                    nc.scalar.activation(feat[h][c][:], feat_ps[h][c][:], ACT.Relu, bias=cb_sb[:, c : c + 1], scale=1.0)
+                else:
+                    nc.vector.tensor_scalar(feat[h][c][:], feat_ps[h][c][:], cb_sb[:, c : c + 1], 0.0, ALU.add, ALU.max)
 
-        z_ps = psum.tile([P, N], F32)
-        for c in range(CH):
-            nc.tensor.matmul(z_ps[:], fc_w_sb[:, c, :], feat[c][:], start=(c == 0), stop=(c == CH - 1))
+        z_ps = [psum.tile([P, H], F32, name=f"z_ps{h}", tag=f"bank{h}") for h in range(HALVES)]
+        for h in range(HALVES):
+            for c in range(CH):
+                nc.tensor.matmul(z_ps[h][:], fc_w_sb[:, c, :], feat[h][c][:], start=(c == 0), stop=(c == CH - 1))
         out_sb = held.tile([P, N], F32)
-        nc.scalar.activation(out_sb[:], z_ps[:], ACT.Relu, bias=shift3[:], scale=scale3[:])
-        nc.sync.dma_start(out, out_sb[:])
+        for h in range(HALVES):
+            nc.scalar.activation(
+                out_sb[:, h * H : (h + 1) * H], z_ps[h][:], ACT.Relu, bias=shift3[:], scale=scale3[:]
+            )
+            nc.sync.dma_start(out[:, h * H : (h + 1) * H], out_sb[:, h * H : (h + 1) * H])

@@ -106,10 +106,6 @@ def tile_conve_kernel(
         nc.gpsimd.tensor_tensor(rstd[:], var_eps[:], minus_half[:], ALU.pow)
         scale3 = held.tile([P, 1], F32)
         nc.gpsimd.tensor_tensor(scale3[:], gain_sb[:], rstd[:], ALU.mult)
-        centred = held.tile([P, 1], F32)
-        nc.gpsimd.tensor_tensor(centred[:], fc_b_sb[:], mean_sb[:], ALU.subtract)
-        shift3 = held.tile([P, 1], F32)
-        nc.gpsimd.tensor_scalar(shift3[:], centred[:], scale3[:], bias_sb[:], ALU.mult, ALU.add)
 
         feat = [[held.tile([P, H], BF16, name=f"feat{h}_{c}") for c in range(CH)] for h in range(HALVES)]
         for h in range(HALVES):
@@ -123,9 +119,10 @@ def tile_conve_kernel(
         for h in range(HALVES):
             for c in range(CH):
                 nc.tensor.matmul(z_ps[h][:], fc_w_sb[:, c, :], feat[h][c][:], start=(c == 0), stop=(c == CH - 1))
+        centred = held.tile([P, N], F32)
         out_sb = held.tile([P, N], F32)
         for h in range(HALVES):
-            nc.scalar.activation(
-                out_sb[:, h * H : (h + 1) * H], z_ps[h][:], ACT.Relu, bias=shift3[:], scale=scale3[:]
-            )
-            nc.sync.dma_start(out[:, h * H : (h + 1) * H], out_sb[:, h * H : (h + 1) * H])
+            half = slice(h * H, (h + 1) * H)
+            nc.vector.tensor_scalar(centred[:, half], z_ps[h][:], fc_b_sb[:], mean_sb[:], ALU.add, ALU.subtract)
+            nc.scalar.activation(out_sb[:, half], centred[:, half], ACT.Relu, bias=bias_sb[:], scale=scale3[:])
+            nc.sync.dma_start(out[:, half], out_sb[:, half])

@@ -68,7 +68,7 @@ def tile_conve_kernel(
 
         zeros = held.tile([P, WARM_COLUMNS], BF16)
         nc.vector.memset(zeros[:], 0.0)
-        warm_ps = psum.tile([P, WARM_COLUMNS], F32, tag="bank4")
+        warm_ps = psum.tile([P, WARM_COLUMNS], F32, tag="bank0")
         for w in range(WARM_MATMULS):
             nc.tensor.matmul(warm_ps[:], zeros[:, 0:P], zeros[:], start=True, stop=True)
 
@@ -77,7 +77,7 @@ def tile_conve_kernel(
 
         tn = held.tile([P, S], BF16)
         for a in range(BLOCKS):
-            flipped = psum.tile([P, P], BF16, name=f"flipped{a}", tag=f"bank{a}")
+            flipped = psum.tile([P, P], BF16, name=f"flipped{a}", tag=f"bank{CH + a}")
             nc.tensor.transpose(flipped[:], table_sb[:, a, :], identity[:])
             if a % 2 == 0:
                 nc.vector.tensor_scalar(tn[:, a * P : (a + 1) * P], flipped[:], S1, SHIFT1, ALU.mult, ALU.add)

@@ -36,10 +36,12 @@ def tile_conve_kernel(
         nc.sync.dma_start(table_sb[:], table.rearrange("(a p) k -> p a k", p=P))
         rel_sb = held.tile([P, N], BF16)
         nc.sync.dma_start(rel_sb[:], rel)
-        w1_sb = held.tile([P, CH * P], BF16)
-        nc.sync.dma_start(w1_sb[:], w1)
         offsets = held.tile([P, N // 16], U16)
         nc.sync.dma_start(offsets[:], offs)
+        var_sb = held.tile([P, 1], F32)
+        nc.sync.dma_start(var_sb[:], bn3_var)
+        w1_sb = held.tile([P, CH * P], BF16)
+        nc.sync.dma_start(w1_sb[:], w1)
         w0_sb = held.tile([P, CH * P], BF16)
         nc.sync.dma_start(w0_sb[:], w0)
         cb_sb = held.tile([P, CH], F32)
@@ -47,14 +49,12 @@ def tile_conve_kernel(
             nc.sync.dma_start(cb_sb[:], cb.rearrange("(c d) o -> d (c o)", d=P))
         fc_w_sb = held.tile([P, CH, P], BF16)
         nc.sync.dma_start(fc_w_sb[:], fc_w.rearrange("(c p) d -> p c d", p=P))
-        var_sb = held.tile([P, 1], F32)
-        nc.sync.dma_start(var_sb[:], bn3_var)
-        gain_sb = held.tile([P, 1], F32)
-        nc.sync.dma_start(gain_sb[:], bn3_gain)
-        mean_sb = held.tile([P, 1], F32)
-        nc.sync.dma_start(mean_sb[:], bn3_mean)
         fc_b_sb = held.tile([P, 1], F32)
         nc.sync.dma_start(fc_b_sb[:], fc_b)
+        mean_sb = held.tile([P, 1], F32)
+        nc.sync.dma_start(mean_sb[:], bn3_mean)
+        gain_sb = held.tile([P, 1], F32)
+        nc.sync.dma_start(gain_sb[:], bn3_gain)
         bias_sb = held.tile([P, 1], F32)
         nc.sync.dma_start(bias_sb[:], bn3_bias)
 
@@ -104,8 +104,12 @@ def tile_conve_kernel(
         nc.gpsimd.tensor_scalar(var_eps[:], var_sb[:], EPS, None, ALU.add)
         rstd = held.tile([P, 1], F32)
         nc.gpsimd.tensor_tensor(rstd[:], var_eps[:], minus_half[:], ALU.pow)
+        centre = held.tile([P, 1], F32)
+        nc.gpsimd.tensor_tensor(centre[:], fc_b_sb[:], mean_sb[:], ALU.subtract)
         scale3 = held.tile([P, 1], F32)
         nc.gpsimd.tensor_tensor(scale3[:], gain_sb[:], rstd[:], ALU.mult)
+        shift3 = held.tile([P, 1], F32)
+        nc.gpsimd.tensor_scalar(shift3[:], scale3[:], centre[:], bias_sb[:], ALU.mult, ALU.add)
 
         feat = [[held.tile([P, H], BF16, name=f"feat{h}_{c}") for c in range(CH)] for h in range(HALVES)]
         for h in range(HALVES):
@@ -119,10 +123,8 @@ def tile_conve_kernel(
         for h in range(HALVES):
             for c in range(CH):
                 nc.tensor.matmul(z_ps[h][:], fc_w_sb[:, c, :], feat[h][c][:], start=(c == 0), stop=(c == CH - 1))
-        centred = held.tile([P, N], F32)
         out_sb = held.tile([P, N], F32)
         for h in range(HALVES):
             half = slice(h * H, (h + 1) * H)
-            nc.vector.tensor_scalar(centred[:, half], z_ps[h][:], fc_b_sb[:], mean_sb[:], ALU.add, ALU.subtract)
-            nc.scalar.activation(out_sb[:, half], centred[:, half], ACT.Relu, bias=bias_sb[:], scale=scale3[:])
+            nc.scalar.activation(out_sb[:, half], z_ps[h][:], ACT.Relu, bias=shift3[:], scale=scale3[:])
             nc.sync.dma_start(out[:, half], out_sb[:, half])

@@ -49,12 +49,12 @@ def tile_conve_kernel(
             nc.sync.dma_start(cb_sb[:], cb.rearrange("(c d) o -> d (c o)", d=P))
         fc_w_sb = held.tile([P, CH, P], BF16)
         nc.sync.dma_start(fc_w_sb[:], fc_w.rearrange("(c p) d -> p c d", p=P))
+        gain_sb = held.tile([P, 1], F32)
+        nc.sync.dma_start(gain_sb[:], bn3_gain)
         fc_b_sb = held.tile([P, 1], F32)
         nc.sync.dma_start(fc_b_sb[:], fc_b)
         mean_sb = held.tile([P, 1], F32)
         nc.sync.dma_start(mean_sb[:], bn3_mean)
-        gain_sb = held.tile([P, 1], F32)
-        nc.sync.dma_start(gain_sb[:], bn3_gain)
         bias_sb = held.tile([P, 1], F32)
         nc.sync.dma_start(bias_sb[:], bn3_bias)
 
@@ -104,12 +104,12 @@ def tile_conve_kernel(
         nc.gpsimd.tensor_scalar(var_eps[:], var_sb[:], EPS, None, ALU.add)
         rstd = held.tile([P, 1], F32)
         nc.gpsimd.tensor_tensor(rstd[:], var_eps[:], minus_half[:], ALU.pow)
-        centre = held.tile([P, 1], F32)
-        nc.gpsimd.tensor_tensor(centre[:], fc_b_sb[:], mean_sb[:], ALU.subtract)
         scale3 = held.tile([P, 1], F32)
         nc.gpsimd.tensor_tensor(scale3[:], gain_sb[:], rstd[:], ALU.mult)
+        centre = held.tile([P, 1], F32)
+        nc.gpsimd.tensor_scalar(centre[:], fc_b_sb[:], mean_sb[:], scale3[:], ALU.subtract, ALU.mult)
         shift3 = held.tile([P, 1], F32)
-        nc.gpsimd.tensor_scalar(shift3[:], scale3[:], centre[:], bias_sb[:], ALU.mult, ALU.add)
+        nc.gpsimd.tensor_tensor(shift3[:], centre[:], bias_sb[:], ALU.add)
 
         feat = [[held.tile([P, H], BF16, name=f"feat{h}_{c}") for c in range(CH)] for h in range(HALVES)]
         for h in range(HALVES):

@@ -13,8 +13,9 @@ EPS = 1e-5
 
 S1 = 1.2 / math.sqrt(0.8 + EPS)
 SHIFT1 = -0.2 * S1 - 0.15
-BLOCKS = S // P
-assert BLOCKS == CH
+PAIR = 2
+GROUPS = S // (P * PAIR)
+assert GROUPS == 2
 WARM_COLUMNS = 512
 WARM_MATMULS = 3
 
@@ -32,8 +33,8 @@ def tile_conve_kernel(
 ):
     nc = tc.nc
     with tc.tile_pool(name="held", bufs=1) as held, tc.psum_pool(name="psum", bufs=1) as psum:
-        table_sb = held.tile([P, BLOCKS, P], BF16)
-        nc.sync.dma_start(table_sb[:], table.rearrange("(a p) k -> p a k", p=P))
+        table_sb = held.tile([P, GROUPS, PAIR, P], BF16)
+        nc.sync.dma_start(table_sb[:], table.rearrange("(g p b) k -> p g b k", g=GROUPS, b=PAIR))
         rel_sb = held.tile([P, N], BF16)
         nc.sync.dma_start(rel_sb[:], rel)
         offsets = held.tile([P, N // 16], U16)
@@ -76,13 +77,16 @@ def tile_conve_kernel(
         nc.gpsimd.tensor_scalar(rn[:], rel_sb[:], S1, SHIFT1, ALU.mult, ALU.add)
 
         tn = held.tile([P, S], BF16)
-        for a in range(BLOCKS):
-            flipped = psum.tile([P, P], BF16, name=f"flipped{a}", tag=f"bank{CH + a}")
-            nc.tensor.transpose(flipped[:], table_sb[:, a, :], identity[:])
-            if a % 2 == 0:
-                nc.vector.tensor_scalar(tn[:, a * P : (a + 1) * P], flipped[:], S1, SHIFT1, ALU.mult, ALU.add)
+        for g in range(GROUPS):
+            flipped = psum.tile([P, PAIR, P], BF16, name=f"flipped{g}", tag=f"bank{CH + g}")
+            for b in range(PAIR):
+                nc.tensor.transpose(flipped[:, b, :], table_sb[:, g, b, :], identity[:])
+            in_node_order = flipped[:].rearrange("k b p -> k p b")
+            columns = tn[:, g * PAIR * P : (g + 1) * PAIR * P].rearrange("k (p b) -> k p b", b=PAIR)
+            if g == 0:
+                nc.vector.tensor_scalar(columns, in_node_order, S1, SHIFT1, ALU.mult, ALU.add)
             else:
-                nc.scalar.activation(tn[:, a * P : (a + 1) * P], flipped[:], ACT.Copy, bias=SHIFT1, scale=S1)
+                nc.scalar.activation(columns, in_node_order, ACT.Copy, bias=SHIFT1, scale=S1)
 
         feat_ps = [
             [psum.tile([P, H], F32, name=f"feat_ps{h}_{c}", tag=f"bank{h * CH + c}") for c in range(CH)]

@@ -59,13 +59,13 @@ def tile_conve_kernel(
         bias_sb = held.tile([P, 1], F32)
         nc.sync.dma_start(bias_sb[:], bn3_bias)
 
-        minus_half = held.tile([P, 1], F32)
-        nc.gpsimd.memset(minus_half[:], -0.5)
+        eps = held.tile([P, 1], F32)
+        nc.gpsimd.memset(eps[:], EPS)
         identity = held.tile([P, P], BF16)
         make_identity(nc, identity[:])
 
         scratch = held.tile([P, 1], F32)
-        nc.scalar.activation(scratch[:], minus_half[:], ACT.Relu)
+        nc.scalar.activation(scratch[:], eps[:], ACT.Abs_reciprocal_sqrt)
 
         zeros = held.tile([P, WARM_COLUMNS], BF16)
         nc.vector.memset(zeros[:], 0.0)
@@ -104,10 +104,8 @@ def tile_conve_kernel(
                     feat_ps[h][c][:], w0_sb[:, c * P : (c + 1) * P], tn[:].indirect(half_offsets), start=False, stop=True
                 )
 
-        var_eps = held.tile([P, 1], F32)
-        nc.gpsimd.tensor_scalar(var_eps[:], var_sb[:], EPS, None, ALU.add)
         rstd = held.tile([P, 1], F32)
-        nc.gpsimd.tensor_tensor(rstd[:], var_eps[:], minus_half[:], ALU.pow)
+        nc.scalar.activation(rstd[:], var_sb[:], ACT.Abs_reciprocal_sqrt, bias=eps[:], scale=1.0)
         scale3 = held.tile([P, 1], F32)
         nc.gpsimd.tensor_tensor(scale3[:], gain_sb[:], rstd[:], ALU.mult)
         centre = held.tile([P, 1], F32)

@@ -16,7 +16,7 @@ SHIFT1 = -0.2 * S1 - 0.15
 PAIR = 2
 GROUPS = S // (P * PAIR)
 assert GROUPS == 2
-WARM_COLUMNS = 512
+WARM_REPEATS = 4
 WARM_MATMULS = 3
 
 FLOPS = 2 * N * P * (CH * P) * 3
@@ -67,14 +67,17 @@ def tile_conve_kernel(
         scratch = held.tile([P, 1], F32)
         nc.scalar.activation(scratch[:], eps[:], ACT.Abs_reciprocal_sqrt)
 
-        zeros = held.tile([P, WARM_COLUMNS], BF16)
+        zeros = held.tile([P, 1, P], BF16)
         nc.vector.memset(zeros[:], 0.0)
-        warm_ps = psum.tile([P, WARM_COLUMNS], F32, tag="bank0")
+        warm_ps = psum.tile([P, WARM_REPEATS, P], F32, tag="bank0")
         for w in range(WARM_MATMULS):
-            nc.tensor.matmul(warm_ps[:], zeros[:, 0:P], zeros[:], start=True, stop=True)
+            nc.tensor.matmul(
+                warm_ps[:], zeros[:, 0, :], zeros[:].to_broadcast([P, WARM_REPEATS, P]), start=True, stop=True
+            )
 
-        rn = held.tile([P, N], BF16)
-        nc.gpsimd.tensor_scalar(rn[:], rel_sb[:], S1, SHIFT1, ALU.mult, ALU.add)
+        rn = [held.tile([P, H], BF16, name=f"rn{h}") for h in range(HALVES)]
+        for h in range(HALVES):
+            nc.gpsimd.tensor_scalar(rn[h][:], rel_sb[:, h * H : (h + 1) * H], S1, SHIFT1, ALU.mult, ALU.add)
 
         tn = held.tile([P, S], BF16)
         for g in range(GROUPS):
@@ -95,7 +98,7 @@ def tile_conve_kernel(
         for h in range(HALVES):
             for c in range(CH):
                 nc.tensor.matmul(
-                    feat_ps[h][c][:], w1_sb[:, c * P : (c + 1) * P], rn[:, h * H : (h + 1) * H], start=True, stop=False
+                    feat_ps[h][c][:], w1_sb[:, c * P : (c + 1) * P], rn[h][:], start=True, stop=False
                 )
         for h in range(HALVES):
             half_offsets = offsets[:, h * (H // 16) : (h + 1) * (H // 16)]

import math

import concourse.mybir as mybir
from concourse.masks import make_identity

P = 128
S = 512
CH = 4
N = 256
HALVES = 2
H = N // HALVES
EPS = 1e-5

S1 = 1.2 / math.sqrt(0.8 + EPS)
SHIFT1 = -0.2 * S1 - 0.15
PAIR = 2
GROUPS = S // (P * PAIR)
assert GROUPS == 2
WARM_REPEATS = 4
WARM_MATMULS = 3

FLOPS = 2 * N * P * (CH * P) * 3

BF16 = mybir.dt.bfloat16
F32 = mybir.dt.float32
U16 = mybir.dt.uint16
ALU = mybir.AluOpType
ACT = mybir.ActivationFunctionType


def tile_conve_kernel(
    tc, table, w0, rel, w1, cb, fc_w, fc_b, bn3_gain, bn3_bias, bn3_mean, bn3_var, offs, out
):
    nc = tc.nc
    with tc.tile_pool(name="held", bufs=1) as held, tc.psum_pool(name="psum", bufs=1) as psum:
        table_sb = held.tile([P, GROUPS, PAIR, P], BF16)
        nc.sync.dma_start(table_sb[:], table.rearrange("(g p b) k -> p g b k", g=GROUPS, b=PAIR))
        rel_sb = held.tile([P, N], BF16)
        nc.sync.dma_start(rel_sb[:], rel)
        offsets = held.tile([P, N // 16], U16)
        nc.sync.dma_start(offsets[:], offs)
        var_sb = held.tile([P, 1], F32)
        nc.sync.dma_start(var_sb[:], bn3_var)
        w1_sb = held.tile([P, CH * P], BF16)
        nc.sync.dma_start(w1_sb[:], w1)
        w0_sb = held.tile([P, CH * P], BF16)
        nc.sync.dma_start(w0_sb[:], w0)
        cb_sb = held.tile([P, CH], F32)
        with nc.allow_non_contiguous_dma(reason="512 biases, one to a partition and block"):
            nc.sync.dma_start(cb_sb[:], cb.rearrange("(c d) o -> d (c o)", d=P))
        fc_w_sb = held.tile([P, CH, P], BF16)
        nc.sync.dma_start(fc_w_sb[:], fc_w.rearrange("(c p) d -> p c d", p=P))
        gain_sb = held.tile([P, 1], F32)
        nc.sync.dma_start(gain_sb[:], bn3_gain)
        fc_b_sb = held.tile([P, 1], F32)
        nc.sync.dma_start(fc_b_sb[:], fc_b)
        mean_sb = held.tile([P, 1], F32)
        nc.sync.dma_start(mean_sb[:], bn3_mean)
        bias_sb = held.tile([P, 1], F32)
        nc.sync.dma_start(bias_sb[:], bn3_bias)

        eps = held.tile([P, 1], F32)
        nc.gpsimd.memset(eps[:], EPS)
        identity = held.tile([P, P], BF16)
        make_identity(nc, identity[:])

        scratch = held.tile([P, 1], F32)
        nc.scalar.activation(scratch[:], eps[:], ACT.Abs_reciprocal_sqrt)

        zeros = held.tile([P, 1, P], BF16)
        nc.vector.memset(zeros[:], 0.0)
        warm_ps = psum.tile([P, WARM_REPEATS, P], F32, tag="bank0")
        for w in range(WARM_MATMULS):
            nc.tensor.matmul(
                warm_ps[:], zeros[:, 0, :], zeros[:].to_broadcast([P, WARM_REPEATS, P]), start=True, stop=True
            )

        rn = [held.tile([P, H], BF16, name=f"rn{h}") for h in range(HALVES)]
        for h in range(HALVES):
            nc.gpsimd.tensor_scalar(rn[h][:], rel_sb[:, h * H : (h + 1) * H], S1, SHIFT1, ALU.mult, ALU.add)

        tn = held.tile([P, S], BF16)
        for g in range(GROUPS):
            flipped = psum.tile([P, PAIR, P], BF16, name=f"flipped{g}", tag=f"bank{CH + g}")
            for b in range(PAIR):
                nc.tensor.transpose(flipped[:, b, :], table_sb[:, g, b, :], identity[:])
            in_node_order = flipped[:].rearrange("k b p -> k p b")
            columns = tn[:, g * PAIR * P : (g + 1) * PAIR * P].rearrange("k (p b) -> k p b", b=PAIR)
            if g == 0:
                nc.vector.tensor_scalar(columns, in_node_order, S1, SHIFT1, ALU.mult, ALU.add)
            else:
                nc.scalar.activation(columns, in_node_order, ACT.Copy, bias=SHIFT1, scale=S1)

        feat_ps = [
            [psum.tile([P, H], F32, name=f"feat_ps{h}_{c}", tag=f"bank{h * CH + c}") for c in range(CH)]
            for h in range(HALVES)
        ]
        for h in range(HALVES):
            for c in range(CH):
                nc.tensor.matmul(
                    feat_ps[h][c][:], w1_sb[:, c * P : (c + 1) * P], rn[h][:], start=True, stop=False
                )
        for h in range(HALVES):
            half_offsets = offsets[:, h * (H // 16) : (h + 1) * (H // 16)]
            for c in range(CH):
                nc.tensor.matmul(
                    feat_ps[h][c][:], w0_sb[:, c * P : (c + 1) * P], tn[:].indirect(half_offsets), start=False, stop=True
                )

        rstd = held.tile([P, 1], F32)
        nc.scalar.activation(rstd[:], var_sb[:], ACT.Abs_reciprocal_sqrt, bias=eps[:], scale=1.0)
        scale3 = held.tile([P, 1], F32)
        nc.gpsimd.tensor_tensor(scale3[:], gain_sb[:], rstd[:], ALU.mult)
        centre = held.tile([P, 1], F32)
        nc.gpsimd.tensor_scalar(centre[:], fc_b_sb[:], mean_sb[:], scale3[:], ALU.subtract, ALU.mult)
        shift3 = held.tile([P, 1], F32)
        nc.gpsimd.tensor_tensor(shift3[:], centre[:], bias_sb[:], ALU.add)

        feat = [[held.tile([P, H], BF16, name=f"feat{h}_{c}") for c in range(CH)] for h in range(HALVES)]
        for h in range(HALVES):
            for c in range(CH):
                if c % 2 == 0:
                    nc.scalar.activation(feat[h][c][:], feat_ps[h][c][:], ACT.Relu, bias=cb_sb[:, c : c + 1], scale=1.0)
                else:
                    nc.vector.tensor_scalar(feat[h][c][:], feat_ps[h][c][:], cb_sb[:, c : c + 1], 0.0, ALU.add, ALU.max)

        z_ps = [psum.tile([P, H], F32, name=f"z_ps{h}", tag=f"bank{h}") for h in range(HALVES)]
        for h in range(HALVES):
            for c in range(CH):
                nc.tensor.matmul(z_ps[h][:], fc_w_sb[:, c, :], feat[h][c][:], start=(c == 0), stop=(c == CH - 1))
        out_sb = held.tile([P, N], F32)
        for h in range(HALVES):
            half = slice(h * H, (h + 1) * H)
            nc.scalar.activation(out_sb[:, half], z_ps[h][:], ACT.Relu, bias=shift3[:], scale=scale3[:])
            nc.sync.dma_start(out[:, half], out_sb[:, half])
